import numpy as np
import ml_dtypes

BF16 = ml_dtypes.bfloat16


def bf(x):
    return np.asarray(x, np.float32).astype(BF16)


def f32(x):
    return np.asarray(x, np.float32)


def f64(x):
    return np.asarray(x).astype(np.float64)


def striped(idx):
    return np.tile(idx.reshape(-1, 16).T, (8, 1))


C, R, S, N, H, K = 128, 128, 2048, 4096, 1024, 4


def ssp(a):
    return np.log(1.0 + np.exp(a)) - np.log(2.0)


def setup_inputs():
    return {"x": f32(np.random.standard_normal((C, S))), "rbf": bf(np.random.uniform(size=(R, N))), "k2f": bf(np.random.standard_normal((R, C)) / np.sqrt(R)), "w_nbr": bf(np.random.standard_normal((C, C)) / np.sqrt(C)), "b_nbr": f32(np.random.standard_normal((C, 1)) / np.sqrt(C)), "offs": striped(np.concatenate([np.random.permutation(S)[:H] for _ in range(K)]))}


def reference(x, rbf, k2f, w_nbr, b_nbr, offs):
    idx = offs[:16].T.reshape(-1)
    xa = ssp(f64(x))
    proj = f64(w_nbr).T @ xa + f64(b_nbr)
    filt = f64(k2f).T @ f64(rbf)
    return proj[:, idx] * filt

@@ -1,0 +1,86 @@
+import math
+
+import concourse.mybir as mybir
+
+F32 = mybir.dt.float32
+BF16 = mybir.dt.bfloat16
+U16 = mybir.dt.uint16
+ALU = mybir.AluOpType
+ACT = mybir.ActivationFunctionType
+
+P = 128
+ATOMS = 2048
+PAIRS = 4096
+BANK = 512
+ATOM_CHUNKS = ATOMS // BANK
+PAIR_PIECES = PAIRS // BANK
+OFFS_PER_COL = 16
+
+LN2 = math.log(2.0)
+EXP_CAP = 30.0
+
+FLOPS = 2 * P * P * (ATOMS + PAIRS)
+
+
+def tile_physnetinteractionlayer_kernel(tc, x, rbf, k2f, w_nbr, b_nbr, offs, out):
+    nc = tc.nc
+    with (
+        tc.tile_pool(name="held", bufs=1) as held,
+        tc.tile_pool(name="chunks", bufs=ATOM_CHUNKS) as chunks,
+        tc.tile_pool(name="pieces", bufs=PAIR_PIECES) as pieces,
+        tc.psum_pool(name="psum", bufs=2) as psum,
+    ):
+        x_chunks = []
+        for c in range(ATOM_CHUNKS):
+            x_chunk = chunks.tile([P, BANK], F32, name="x_chunk")
+            queue = nc.sync if c % 2 == 0 else nc.scalar
+            queue.dma_start(x_chunk[:], x[:, c * BANK : (c + 1) * BANK])
+            x_chunks.append(x_chunk)
+
+        w_sb = held.tile([P, P], BF16, name="w_sb")
+        nc.gpsimd.dma_start(w_sb[:], w_nbr)
+        bias = held.tile([P, 1], F32, name="bias")
+        nc.gpsimd.dma_start(bias[:], b_nbr)
+        k2f_sb = held.tile([P, P], BF16, name="k2f_sb")
+        nc.gpsimd.dma_start(k2f_sb[:], k2f)
+
+        offsets = held.tile([P, PAIRS // OFFS_PER_COL], U16, name="offsets")
+        nc.sync.dma_start(offsets[:], offs)
+
+        rbf_sb = held.tile([P, PAIRS], BF16, name="rbf_sb")
+        rbf_part = PAIRS // 4
+        for r in range(4):
+            queue = nc.sync if r % 2 == 0 else nc.scalar
+            queue.dma_start(
+                rbf_sb[:, r * rbf_part : (r + 1) * rbf_part],
+                rbf[:, r * rbf_part : (r + 1) * rbf_part],
+            )
+
+        proj = held.tile([P, ATOMS], F32, name="proj")
+        for c in range(ATOM_CHUNKS):
+            x_chunk = x_chunks[c]
+            capped = chunks.tile([P, BANK], F32, name="capped")
+            nc.vector.tensor_scalar_min(capped[:], x_chunk[:], EXP_CAP)
+            grown = chunks.tile([P, BANK], F32, name="grown")
+            nc.scalar.activation(grown[:], capped[:], ACT.Exp)
+            logged = chunks.tile([P, BANK], F32, name="logged")
+            nc.scalar.activation(logged[:], grown[:], ACT.Ln, bias=0.5, scale=0.5)
+            xa = chunks.tile([P, BANK], BF16, name="xa")
+            nc.vector.scalar_tensor_tensor(xa[:], x_chunk[:], -LN2, logged[:], ALU.add, ALU.max)
+
+            proj_ps = psum.tile([P, BANK], F32, name="proj_ps")
+            nc.tensor.matmul(proj_ps[:], w_sb[:], xa[:], start=True, stop=True)
+            nc.vector.tensor_scalar_add(proj[:, c * BANK : (c + 1) * BANK], proj_ps[:], bias[:, 0:1])
+
+        for k in range(PAIR_PIECES):
+            filt_ps = psum.tile([P, BANK], F32, name="filt_ps")
+            nc.tensor.matmul(filt_ps[:], k2f_sb[:], rbf_sb[:, k * BANK : (k + 1) * BANK], start=True, stop=True)
+            filt = pieces.tile([P, BANK], F32, name="filt")
+            nc.scalar.copy(filt[:], filt_ps[:])
+
+            cols = BANK // OFFS_PER_COL
+            message = pieces.tile([P, BANK], F32, name="message")
+            nc.vector.tensor_tensor(
+                message[:], proj[:].indirect(offsets[:, k * cols : (k + 1) * cols]), filt[:], ALU.mult
+            )
+            nc.sync.dma_start(out[:, k * BANK : (k + 1) * BANK], message[:])

@@ -28,21 +28,13 @@ def tile_physnetinteractionlayer_kernel(tc, x, rbf, k2f, w_nbr, b_nbr, offs, out
         tc.tile_pool(name="held", bufs=1) as held,
         tc.tile_pool(name="chunks", bufs=ATOM_CHUNKS) as chunks,
         tc.tile_pool(name="pieces", bufs=PAIR_PIECES) as pieces,
-        tc.psum_pool(name="psum", bufs=2) as psum,
+        tc.psum_pool(name="psum", bufs=4) as psum,
     ):
         x_chunks = []
         for c in range(ATOM_CHUNKS):
             x_chunk = chunks.tile([P, BANK], F32, name="x_chunk")
-            queue = nc.sync if c % 2 == 0 else nc.scalar
-            queue.dma_start(x_chunk[:], x[:, c * BANK : (c + 1) * BANK])
+            nc.sync.dma_start(x_chunk[:], x[:, c * BANK : (c + 1) * BANK])
             x_chunks.append(x_chunk)
-
-        w_sb = held.tile([P, P], BF16, name="w_sb")
-        nc.gpsimd.dma_start(w_sb[:], w_nbr)
-        bias = held.tile([P, 1], F32, name="bias")
-        nc.gpsimd.dma_start(bias[:], b_nbr)
-        k2f_sb = held.tile([P, P], BF16, name="k2f_sb")
-        nc.gpsimd.dma_start(k2f_sb[:], k2f)
 
         offsets = held.tile([P, PAIRS // OFFS_PER_COL], U16, name="offsets")
         nc.sync.dma_start(offsets[:], offs)
@@ -50,33 +42,49 @@ def tile_physnetinteractionlayer_kernel(tc, x, rbf, k2f, w_nbr, b_nbr, offs, out
         rbf_sb = held.tile([P, PAIRS], BF16, name="rbf_sb")
         rbf_part = PAIRS // 4
         for r in range(4):
-            queue = nc.sync if r % 2 == 0 else nc.scalar
-            queue.dma_start(
+            nc.sync.dma_start(
                 rbf_sb[:, r * rbf_part : (r + 1) * rbf_part],
                 rbf[:, r * rbf_part : (r + 1) * rbf_part],
             )
 
-        proj = held.tile([P, ATOMS], F32, name="proj")
+        w_sb = held.tile([P, P], BF16, name="w_sb")
+        nc.scalar.dma_start(w_sb[:], w_nbr)
+        bias = held.tile([P, 1], F32, name="bias")
+        nc.scalar.dma_start(bias[:], b_nbr)
+        k2f_sb = held.tile([P, P], BF16, name="k2f_sb")
+        nc.scalar.dma_start(k2f_sb[:], k2f)
+
+        grown_chunks = []
         for c in range(ATOM_CHUNKS):
-            x_chunk = x_chunks[c]
             capped = chunks.tile([P, BANK], F32, name="capped")
-            nc.vector.tensor_scalar_min(capped[:], x_chunk[:], EXP_CAP)
+            nc.vector.tensor_scalar_min(capped[:], x_chunks[c][:], EXP_CAP)
             grown = chunks.tile([P, BANK], F32, name="grown")
             nc.scalar.activation(grown[:], capped[:], ACT.Exp)
+            grown_chunks.append(grown)
+
+        proj = held.tile([P, ATOMS], F32, name="proj")
+        for c in range(ATOM_CHUNKS):
             logged = chunks.tile([P, BANK], F32, name="logged")
-            nc.scalar.activation(logged[:], grown[:], ACT.Ln, bias=0.5, scale=0.5)
+            nc.scalar.activation(logged[:], grown_chunks[c][:], ACT.Ln, bias=0.5, scale=0.5)
             xa = chunks.tile([P, BANK], BF16, name="xa")
-            nc.vector.scalar_tensor_tensor(xa[:], x_chunk[:], -LN2, logged[:], ALU.add, ALU.max)
+            nc.vector.scalar_tensor_tensor(xa[:], x_chunks[c][:], -LN2, logged[:], ALU.add, ALU.max)
 
             proj_ps = psum.tile([P, BANK], F32, name="proj_ps")
             nc.tensor.matmul(proj_ps[:], w_sb[:], xa[:], start=True, stop=True)
-            nc.vector.tensor_scalar_add(proj[:, c * BANK : (c + 1) * BANK], proj_ps[:], bias[:, 0:1])
+            proj_chunk = proj[:, c * BANK : (c + 1) * BANK]
+            if c < ATOM_CHUNKS // 2:
+                nc.scalar.activation(proj_chunk, proj_ps[:], ACT.Identity, bias=bias[:, 0:1])
+            else:
+                nc.vector.tensor_scalar_add(proj_chunk, proj_ps[:], bias[:, 0:1])
 
         for k in range(PAIR_PIECES):
             filt_ps = psum.tile([P, BANK], F32, name="filt_ps")
             nc.tensor.matmul(filt_ps[:], k2f_sb[:], rbf_sb[:, k * BANK : (k + 1) * BANK], start=True, stop=True)
             filt = pieces.tile([P, BANK], F32, name="filt")
-            nc.scalar.copy(filt[:], filt_ps[:])
+            if k < PAIR_PIECES // 2:
+                nc.vector.tensor_copy(filt[:], filt_ps[:])
+            else:
+                nc.scalar.copy(filt[:], filt_ps[:])
 
             cols = BANK // OFFS_PER_COL
             message = pieces.tile([P, BANK], F32, name="message")

@@ -11,9 +11,13 @@ ACT = mybir.ActivationFunctionType
 P = 128
 ATOMS = 2048
 PAIRS = 4096
-BANK = 512
-ATOM_CHUNKS = ATOMS // BANK
-PAIR_PIECES = PAIRS // BANK
+LOAD = 512
+CHUNK = 256
+PIECE = 512
+ATOM_LOADS = ATOMS // LOAD
+ATOM_CHUNKS = ATOMS // CHUNK
+PAIR_PIECES = PAIRS // PIECE
+EARLY_PIECES = 2
 OFFS_PER_COL = 16
 
 LN2 = math.log(2.0)
@@ -28,24 +32,23 @@ def tile_physnetinteractionlayer_kernel(tc, x, rbf, k2f, w_nbr, b_nbr, offs, out
         tc.tile_pool(name="held", bufs=1) as held,
         tc.tile_pool(name="chunks", bufs=ATOM_CHUNKS) as chunks,
         tc.tile_pool(name="pieces", bufs=PAIR_PIECES) as pieces,
-        tc.psum_pool(name="psum", bufs=4) as psum,
+        tc.psum_pool(name="psum_vector", bufs=4) as psum_vector,
+        tc.psum_pool(name="psum_scalar", bufs=4) as psum_scalar,
     ):
-        x_chunks = []
-        for c in range(ATOM_CHUNKS):
-            x_chunk = chunks.tile([P, BANK], F32, name="x_chunk")
-            nc.sync.dma_start(x_chunk[:], x[:, c * BANK : (c + 1) * BANK])
-            x_chunks.append(x_chunk)
-
-        offsets = held.tile([P, PAIRS // OFFS_PER_COL], U16, name="offsets")
-        nc.sync.dma_start(offsets[:], offs)
+        x_sb = held.tile([P, ATOMS], F32, name="x_sb")
+        for a in range(ATOM_LOADS):
+            nc.sync.dma_start(x_sb[:, a * LOAD : (a + 1) * LOAD], x[:, a * LOAD : (a + 1) * LOAD])
 
         rbf_sb = held.tile([P, PAIRS], BF16, name="rbf_sb")
+        offsets = held.tile([P, PAIRS // OFFS_PER_COL], U16, name="offsets")
         rbf_part = PAIRS // 4
         for r in range(4):
             nc.sync.dma_start(
                 rbf_sb[:, r * rbf_part : (r + 1) * rbf_part],
                 rbf[:, r * rbf_part : (r + 1) * rbf_part],
             )
+            if r == 0:
+                nc.sync.dma_start(offsets[:], offs)
 
         w_sb = held.tile([P, P], BF16, name="w_sb")
         nc.scalar.dma_start(w_sb[:], w_nbr)
@@ -54,41 +57,54 @@ def tile_physnetinteractionlayer_kernel(tc, x, rbf, k2f, w_nbr, b_nbr, offs, out
         k2f_sb = held.tile([P, P], BF16, name="k2f_sb")
         nc.scalar.dma_start(k2f_sb[:], k2f)
 
-        grown_chunks = []
+        capped = held.tile([P, ATOMS], F32, name="capped")
+        grown = held.tile([P, ATOMS], F32, name="grown")
+        line = held.tile([P, ATOMS], BF16, name="line")
+        for a in range(ATOM_LOADS):
+            part = slice(a * LOAD, (a + 1) * LOAD)
+            nc.vector.tensor_scalar_min(capped[:, part], x_sb[:, part], EXP_CAP)
+            nc.scalar.activation(grown[:, part], capped[:, part], ACT.Exp)
+            nc.vector.tensor_scalar_add(line[:, part], x_sb[:, part], -LN2)
+
+        filt_pieces = []
+        for k in range(EARLY_PIECES):
+            filt_ps = psum_vector.tile([P, PIECE], F32, name="bank")
+            nc.tensor.matmul(filt_ps[:], k2f_sb[:], rbf_sb[:, k * PIECE : (k + 1) * PIECE], start=True, stop=True)
+            filt = pieces.tile([P, PIECE], F32, name="filt")
+            nc.vector.tensor_copy(filt[:], filt_ps[:])
+            filt_pieces.append(filt)
+
+        proj_ps_chunks = []
         for c in range(ATOM_CHUNKS):
-            capped = chunks.tile([P, BANK], F32, name="capped")
-            nc.vector.tensor_scalar_min(capped[:], x_chunks[c][:], EXP_CAP)
-            grown = chunks.tile([P, BANK], F32, name="grown")
-            nc.scalar.activation(grown[:], capped[:], ACT.Exp)
-            grown_chunks.append(grown)
+            chunk = slice(c * CHUNK, (c + 1) * CHUNK)
+            logged = chunks.tile([P, CHUNK], BF16, name="logged")
+            nc.scalar.activation(logged[:], grown[:, chunk], ACT.Ln, bias=0.5, scale=0.5)
+            xa = chunks.tile([P, CHUNK], BF16, name="xa")
+            nc.vector.tensor_tensor(xa[:], logged[:], line[:, chunk], ALU.max)
+            psum = psum_vector if c < ATOM_CHUNKS // 2 else psum_scalar
+            proj_ps = psum.tile([P, CHUNK], F32, name="bank")
+            nc.tensor.matmul(proj_ps[:], w_sb[:], xa[:], start=True, stop=True)
+            proj_ps_chunks.append(proj_ps)
 
         proj = held.tile([P, ATOMS], F32, name="proj")
         for c in range(ATOM_CHUNKS):
-            logged = chunks.tile([P, BANK], F32, name="logged")
-            nc.scalar.activation(logged[:], grown_chunks[c][:], ACT.Ln, bias=0.5, scale=0.5)
-            xa = chunks.tile([P, BANK], BF16, name="xa")
-            nc.vector.scalar_tensor_tensor(xa[:], x_chunks[c][:], -LN2, logged[:], ALU.add, ALU.max)
-
-            proj_ps = psum.tile([P, BANK], F32, name="proj_ps")
-            nc.tensor.matmul(proj_ps[:], w_sb[:], xa[:], start=True, stop=True)
-            proj_chunk = proj[:, c * BANK : (c + 1) * BANK]
+            chunk = slice(c * CHUNK, (c + 1) * CHUNK)
             if c < ATOM_CHUNKS // 2:
-                nc.scalar.activation(proj_chunk, proj_ps[:], ACT.Identity, bias=bias[:, 0:1])
+                nc.vector.tensor_scalar_add(proj[:, chunk], proj_ps_chunks[c][:], bias[:, 0:1])
             else:
-                nc.vector.tensor_scalar_add(proj_chunk, proj_ps[:], bias[:, 0:1])
+                nc.scalar.activation(proj[:, chunk], proj_ps_chunks[c][:], ACT.Identity, bias=bias[:, 0:1])
 
+        for k in range(EARLY_PIECES, PAIR_PIECES):
+            filt_ps = psum_scalar.tile([P, PIECE], F32, name="bank")
+            nc.tensor.matmul(filt_ps[:], k2f_sb[:], rbf_sb[:, k * PIECE : (k + 1) * PIECE], start=True, stop=True)
+            filt = pieces.tile([P, PIECE], F32, name="filt")
+            nc.scalar.copy(filt[:], filt_ps[:])
+            filt_pieces.append(filt)
+
+        cols = PIECE // OFFS_PER_COL
         for k in range(PAIR_PIECES):
-            filt_ps = psum.tile([P, BANK], F32, name="filt_ps")
-            nc.tensor.matmul(filt_ps[:], k2f_sb[:], rbf_sb[:, k * BANK : (k + 1) * BANK], start=True, stop=True)
-            filt = pieces.tile([P, BANK], F32, name="filt")
-            if k < PAIR_PIECES // 2:
-                nc.vector.tensor_copy(filt[:], filt_ps[:])
-            else:
-                nc.scalar.copy(filt[:], filt_ps[:])
-
-            cols = BANK // OFFS_PER_COL
-            message = pieces.tile([P, BANK], F32, name="message")
+            message = pieces.tile([P, PIECE], F32, name="message")
             nc.vector.tensor_tensor(
-                message[:], proj[:].indirect(offsets[:, k * cols : (k + 1) * cols]), filt[:], ALU.mult
+                message[:], proj[:].indirect(offsets[:, k * cols : (k + 1) * cols]), filt_pieces[k][:], ALU.mult
             )
-            nc.sync.dma_start(out[:, k * BANK : (k + 1) * BANK], message[:])
+            nc.sync.dma_start(out[:, k * PIECE : (k + 1) * PIECE], message[:])

@@ -13,15 +13,18 @@ ATOMS = 2048
 PAIRS = 4096
 LOAD = 512
 CHUNK = 256
-PIECE = 512
+BANK = 512
+PIECE = BANK
 ATOM_LOADS = ATOMS // LOAD
 ATOM_CHUNKS = ATOMS // CHUNK
 PAIR_PIECES = PAIRS // PIECE
+ATOM_BANKS = ATOMS // BANK
+CHUNKS_PER_BANK = BANK // CHUNK
 EARLY_PIECES = 2
 OFFS_PER_COL = 16
 
 LN2 = math.log(2.0)
-EXP_CAP = 30.0
+EXP_CAP = math.exp(30.0)
 
 FLOPS = 2 * P * P * (ATOMS + PAIRS)
 
@@ -32,8 +35,8 @@ def tile_physnetinteractionlayer_kernel(tc, x, rbf, k2f, w_nbr, b_nbr, offs, out
         tc.tile_pool(name="held", bufs=1) as held,
         tc.tile_pool(name="chunks", bufs=ATOM_CHUNKS) as chunks,
         tc.tile_pool(name="pieces", bufs=PAIR_PIECES) as pieces,
-        tc.psum_pool(name="psum_vector", bufs=4) as psum_vector,
-        tc.psum_pool(name="psum_scalar", bufs=4) as psum_scalar,
+        tc.psum_pool(name="psum_proj", bufs=ATOM_BANKS) as psum_proj,
+        tc.psum_pool(name="psum_filt", bufs=4) as psum_filt,
     ):
         x_sb = held.tile([P, ATOMS], F32, name="x_sb")
         for a in range(ATOM_LOADS):
@@ -57,54 +60,60 @@ def tile_physnetinteractionlayer_kernel(tc, x, rbf, k2f, w_nbr, b_nbr, offs, out
         k2f_sb = held.tile([P, P], BF16, name="k2f_sb")
         nc.scalar.dma_start(k2f_sb[:], k2f)
 
-        capped = held.tile([P, ATOMS], F32, name="capped")
         grown = held.tile([P, ATOMS], F32, name="grown")
+        capped = held.tile([P, ATOMS], F32, name="capped")
         line = held.tile([P, ATOMS], BF16, name="line")
         for a in range(ATOM_LOADS):
             part = slice(a * LOAD, (a + 1) * LOAD)
-            nc.vector.tensor_scalar_min(capped[:, part], x_sb[:, part], EXP_CAP)
-            nc.scalar.activation(grown[:, part], capped[:, part], ACT.Exp)
+            nc.scalar.activation(grown[:, part], x_sb[:, part], ACT.Exp)
+            nc.vector.tensor_scalar_min(capped[:, part], grown[:, part], EXP_CAP)
             nc.vector.tensor_scalar_add(line[:, part], x_sb[:, part], -LN2)
 
         filt_pieces = []
         for k in range(EARLY_PIECES):
-            filt_ps = psum_vector.tile([P, PIECE], F32, name="bank")
+            filt_ps = psum_filt.tile([P, PIECE], F32, name="filt_ps")
             nc.tensor.matmul(filt_ps[:], k2f_sb[:], rbf_sb[:, k * PIECE : (k + 1) * PIECE], start=True, stop=True)
             filt = pieces.tile([P, PIECE], F32, name="filt")
             nc.vector.tensor_copy(filt[:], filt_ps[:])
             filt_pieces.append(filt)
 
-        proj_ps_chunks = []
-        for c in range(ATOM_CHUNKS):
-            chunk = slice(c * CHUNK, (c + 1) * CHUNK)
-            logged = chunks.tile([P, CHUNK], BF16, name="logged")
-            nc.scalar.activation(logged[:], grown[:, chunk], ACT.Ln, bias=0.5, scale=0.5)
-            xa = chunks.tile([P, CHUNK], BF16, name="xa")
-            nc.vector.tensor_tensor(xa[:], logged[:], line[:, chunk], ALU.max)
-            psum = psum_vector if c < ATOM_CHUNKS // 2 else psum_scalar
-            proj_ps = psum.tile([P, CHUNK], F32, name="bank")
-            nc.tensor.matmul(proj_ps[:], w_sb[:], xa[:], start=True, stop=True)
-            proj_ps_chunks.append(proj_ps)
+        proj_banks = []
+        for b in range(ATOM_BANKS):
+            proj_ps = psum_proj.tile([P, BANK], F32, name="proj_ps")
+            for h in range(CHUNKS_PER_BANK):
+                first = b * BANK + h * CHUNK
+                logged = chunks.tile([P, CHUNK], BF16, name="logged")
+                nc.scalar.activation(logged[:], capped[:, first : first + CHUNK], ACT.Ln, bias=0.5, scale=0.5)
+                xa = chunks.tile([P, CHUNK], BF16, name="xa")
+                nc.vector.tensor_tensor(xa[:], logged[:], line[:, first : first + CHUNK], ALU.max)
+                nc.tensor.matmul(proj_ps[:, h * CHUNK : (h + 1) * CHUNK], w_sb[:], xa[:], start=True, stop=True)
+            proj_banks.append(proj_ps)
 
         proj = held.tile([P, ATOMS], F32, name="proj")
-        for c in range(ATOM_CHUNKS):
-            chunk = slice(c * CHUNK, (c + 1) * CHUNK)
-            if c < ATOM_CHUNKS // 2:
-                nc.vector.tensor_scalar_add(proj[:, chunk], proj_ps_chunks[c][:], bias[:, 0:1])
+        for b in range(ATOM_BANKS):
+            proj_part = proj[:, b * BANK : (b + 1) * BANK]
+            if b < ATOM_BANKS // 2:
+                nc.scalar.activation(proj_part, proj_banks[b][:], ACT.Identity, bias=bias[:, 0:1])
             else:
-                nc.scalar.activation(proj[:, chunk], proj_ps_chunks[c][:], ACT.Identity, bias=bias[:, 0:1])
+                nc.vector.tensor_scalar_add(proj_part, proj_banks[b][:], bias[:, 0:1])
 
         for k in range(EARLY_PIECES, PAIR_PIECES):
-            filt_ps = psum_scalar.tile([P, PIECE], F32, name="bank")
+            filt_ps = psum_filt.tile([P, PIECE], F32, name="filt_ps")
             nc.tensor.matmul(filt_ps[:], k2f_sb[:], rbf_sb[:, k * PIECE : (k + 1) * PIECE], start=True, stop=True)
             filt = pieces.tile([P, PIECE], F32, name="filt")
             nc.scalar.copy(filt[:], filt_ps[:])
             filt_pieces.append(filt)
 
-        cols = PIECE // OFFS_PER_COL
         for k in range(PAIR_PIECES):
             message = pieces.tile([P, PIECE], F32, name="message")
-            nc.vector.tensor_tensor(
-                message[:], proj[:].indirect(offsets[:, k * cols : (k + 1) * cols]), filt_pieces[k][:], ALU.mult
-            )
-            nc.sync.dma_start(out[:, k * PIECE : (k + 1) * PIECE], message[:])
+            cuts = 2 if k == PAIR_PIECES - 1 else 1
+            width = PIECE // cuts
+            for h in range(cuts):
+                first = k * PIECE + h * width
+                nc.vector.tensor_tensor(
+                    message[:, h * width : (h + 1) * width],
+                    proj[:].indirect(offsets[:, first // OFFS_PER_COL : (first + width) // OFFS_PER_COL]),
+                    filt_pieces[k][:, h * width : (h + 1) * width],
+                    ALU.mult,
+                )
+                nc.sync.dma_start(out[:, first : first + width], message[:, h * width : (h + 1) * width])

@@ -18,13 +18,11 @@ PIECE = BANK
 ATOM_LOADS = ATOMS // LOAD
 ATOM_CHUNKS = ATOMS // CHUNK
 PAIR_PIECES = PAIRS // PIECE
-ATOM_BANKS = ATOMS // BANK
-CHUNKS_PER_BANK = BANK // CHUNK
 EARLY_PIECES = 2
 OFFS_PER_COL = 16
 
-LN2 = math.log(2.0)
-EXP_CAP = math.exp(30.0)
+KNEE = 30.0
+EXP_CAP = math.exp(KNEE)
 
 FLOPS = 2 * P * P * (ATOMS + PAIRS)
 
@@ -35,7 +33,7 @@ def tile_physnetinteractionlayer_kernel(tc, x, rbf, k2f, w_nbr, b_nbr, offs, out
         tc.tile_pool(name="held", bufs=1) as held,
         tc.tile_pool(name="chunks", bufs=ATOM_CHUNKS) as chunks,
         tc.tile_pool(name="pieces", bufs=PAIR_PIECES) as pieces,
-        tc.psum_pool(name="psum_proj", bufs=ATOM_BANKS) as psum_proj,
+        tc.psum_pool(name="psum_proj", bufs=4) as psum_proj,
         tc.psum_pool(name="psum_filt", bufs=4) as psum_filt,
     ):
         x_sb = held.tile([P, ATOMS], F32, name="x_sb")
@@ -62,12 +60,12 @@ def tile_physnetinteractionlayer_kernel(tc, x, rbf, k2f, w_nbr, b_nbr, offs, out
 
         grown = held.tile([P, ATOMS], F32, name="grown")
         capped = held.tile([P, ATOMS], F32, name="capped")
-        line = held.tile([P, ATOMS], BF16, name="line")
+        excess = held.tile([P, ATOMS], BF16, name="excess")
         for a in range(ATOM_LOADS):
             part = slice(a * LOAD, (a + 1) * LOAD)
             nc.scalar.activation(grown[:, part], x_sb[:, part], ACT.Exp)
+            nc.vector.tensor_scalar(excess[:, part], x_sb[:, part], -KNEE, 0.0, op0=ALU.add, op1=ALU.max)
             nc.vector.tensor_scalar_min(capped[:, part], grown[:, part], EXP_CAP)
-            nc.vector.tensor_scalar_add(line[:, part], x_sb[:, part], -LN2)
 
         filt_pieces = []
         for k in range(EARLY_PIECES):
@@ -77,25 +75,15 @@ def tile_physnetinteractionlayer_kernel(tc, x, rbf, k2f, w_nbr, b_nbr, offs, out
             nc.vector.tensor_copy(filt[:], filt_ps[:])
             filt_pieces.append(filt)
 
-        proj_banks = []
-        for b in range(ATOM_BANKS):
-            proj_ps = psum_proj.tile([P, BANK], F32, name="proj_ps")
-            for h in range(CHUNKS_PER_BANK):
-                first = b * BANK + h * CHUNK
-                logged = chunks.tile([P, CHUNK], BF16, name="logged")
-                nc.scalar.activation(logged[:], capped[:, first : first + CHUNK], ACT.Ln, bias=0.5, scale=0.5)
-                xa = chunks.tile([P, CHUNK], BF16, name="xa")
-                nc.vector.tensor_tensor(xa[:], logged[:], line[:, first : first + CHUNK], ALU.max)
-                nc.tensor.matmul(proj_ps[:, h * CHUNK : (h + 1) * CHUNK], w_sb[:], xa[:], start=True, stop=True)
-            proj_banks.append(proj_ps)
-
         proj = held.tile([P, ATOMS], F32, name="proj")
-        for b in range(ATOM_BANKS):
-            proj_part = proj[:, b * BANK : (b + 1) * BANK]
-            if b < ATOM_BANKS // 2:
-                nc.scalar.activation(proj_part, proj_banks[b][:], ACT.Identity, bias=bias[:, 0:1])
-            else:
-                nc.vector.tensor_scalar_add(proj_part, proj_banks[b][:], bias[:, 0:1])
+        for c in range(ATOM_CHUNKS):
+            chunk = slice(c * CHUNK, (c + 1) * CHUNK)
+            logged = chunks.tile([P, CHUNK], BF16, name="logged")
+            nc.scalar.activation(logged[:], capped[:, chunk], ACT.Ln, bias=0.5, scale=0.5)
+            proj_ps = psum_proj.tile([P, CHUNK], F32, name="proj_ps")
+            nc.tensor.matmul(proj_ps[:], w_sb[:], excess[:, chunk], start=True, stop=False)
+            nc.tensor.matmul(proj_ps[:], w_sb[:], logged[:], start=False, stop=True)
+            nc.vector.tensor_scalar_add(proj[:, chunk], proj_ps[:], bias[:, 0:1])
 
         for k in range(EARLY_PIECES, PAIR_PIECES):
             filt_ps = psum_filt.tile([P, PIECE], F32, name="filt_ps")

import math

import concourse.mybir as mybir

F32 = mybir.dt.float32
BF16 = mybir.dt.bfloat16
U16 = mybir.dt.uint16
ALU = mybir.AluOpType
ACT = mybir.ActivationFunctionType

P = 128
ATOMS = 2048
PAIRS = 4096
LOAD = 512
CHUNK = 256
BANK = 512
PIECE = BANK
ATOM_LOADS = ATOMS // LOAD
ATOM_CHUNKS = ATOMS // CHUNK
PAIR_PIECES = PAIRS // PIECE
EARLY_PIECES = 2
OFFS_PER_COL = 16

KNEE = 30.0
EXP_CAP = math.exp(KNEE)

FLOPS = 2 * P * P * (ATOMS + PAIRS)


def tile_physnetinteractionlayer_kernel(tc, x, rbf, k2f, w_nbr, b_nbr, offs, out):
    nc = tc.nc
    with (
        tc.tile_pool(name="held", bufs=1) as held,
        tc.tile_pool(name="chunks", bufs=ATOM_CHUNKS) as chunks,
        tc.tile_pool(name="pieces", bufs=PAIR_PIECES) as pieces,
        tc.psum_pool(name="psum_proj", bufs=4) as psum_proj,
        tc.psum_pool(name="psum_filt", bufs=4) as psum_filt,
    ):
        x_sb = held.tile([P, ATOMS], F32, name="x_sb")
        for a in range(ATOM_LOADS):
            nc.sync.dma_start(x_sb[:, a * LOAD : (a + 1) * LOAD], x[:, a * LOAD : (a + 1) * LOAD])

        rbf_sb = held.tile([P, PAIRS], BF16, name="rbf_sb")
        offsets = held.tile([P, PAIRS // OFFS_PER_COL], U16, name="offsets")
        rbf_part = PAIRS // 4
        for r in range(4):
            nc.sync.dma_start(
                rbf_sb[:, r * rbf_part : (r + 1) * rbf_part],
                rbf[:, r * rbf_part : (r + 1) * rbf_part],
            )
            if r == 0:
                nc.sync.dma_start(offsets[:], offs)

        w_sb = held.tile([P, P], BF16, name="w_sb")
        nc.scalar.dma_start(w_sb[:], w_nbr)
        bias = held.tile([P, 1], F32, name="bias")
        nc.scalar.dma_start(bias[:], b_nbr)
        k2f_sb = held.tile([P, P], BF16, name="k2f_sb")
        nc.scalar.dma_start(k2f_sb[:], k2f)

        grown = held.tile([P, ATOMS], F32, name="grown")
        capped = held.tile([P, ATOMS], F32, name="capped")
        excess = held.tile([P, ATOMS], BF16, name="excess")
        for a in range(ATOM_LOADS):
            part = slice(a * LOAD, (a + 1) * LOAD)
            nc.scalar.activation(grown[:, part], x_sb[:, part], ACT.Exp)
            nc.vector.tensor_scalar(excess[:, part], x_sb[:, part], -KNEE, 0.0, op0=ALU.add, op1=ALU.max)
            nc.vector.tensor_scalar_min(capped[:, part], grown[:, part], EXP_CAP)

        filt_pieces = []
        for k in range(EARLY_PIECES):
            filt_ps = psum_filt.tile([P, PIECE], F32, name="filt_ps")
            nc.tensor.matmul(filt_ps[:], k2f_sb[:], rbf_sb[:, k * PIECE : (k + 1) * PIECE], start=True, stop=True)
            filt = pieces.tile([P, PIECE], F32, name="filt")
            nc.vector.tensor_copy(filt[:], filt_ps[:])
            filt_pieces.append(filt)

        proj = held.tile([P, ATOMS], F32, name="proj")
        for c in range(ATOM_CHUNKS):
            chunk = slice(c * CHUNK, (c + 1) * CHUNK)
            logged = chunks.tile([P, CHUNK], BF16, name="logged")
            nc.scalar.activation(logged[:], capped[:, chunk], ACT.Ln, bias=0.5, scale=0.5)
            proj_ps = psum_proj.tile([P, CHUNK], F32, name="proj_ps")
            nc.tensor.matmul(proj_ps[:], w_sb[:], excess[:, chunk], start=True, stop=False)
            nc.tensor.matmul(proj_ps[:], w_sb[:], logged[:], start=False, stop=True)
            nc.vector.tensor_scalar_add(proj[:, chunk], proj_ps[:], bias[:, 0:1])

        for k in range(EARLY_PIECES, PAIR_PIECES):
            filt_ps = psum_filt.tile([P, PIECE], F32, name="filt_ps")
            nc.tensor.matmul(filt_ps[:], k2f_sb[:], rbf_sb[:, k * PIECE : (k + 1) * PIECE], start=True, stop=True)
            filt = pieces.tile([P, PIECE], F32, name="filt")
            nc.scalar.copy(filt[:], filt_ps[:])
            filt_pieces.append(filt)

        for k in range(PAIR_PIECES):
            message = pieces.tile([P, PIECE], F32, name="message")
            cuts = 2 if k == PAIR_PIECES - 1 else 1
            width = PIECE // cuts
            for h in range(cuts):
                first = k * PIECE + h * width
                nc.vector.tensor_tensor(
                    message[:, h * width : (h + 1) * width],
                    proj[:].indirect(offsets[:, first // OFFS_PER_COL : (first + width) // OFFS_PER_COL]),
                    filt_pieces[k][:, h * width : (h + 1) * width],
                    ALU.mult,
                )
                nc.sync.dma_start(out[:, first : first + width], message[:, h * width : (h + 1) * width])
